import numpy as np
import ml_dtypes


def mxq(x, axis, fmt="e4m3"):
    dtype, down = {"e4m3": (ml_dtypes.float8_e4m3fn, 7), "e5m2": (ml_dtypes.float8_e5m2, 14)}[fmt]
    v = np.moveaxis(np.asarray(x, np.float32).astype(ml_dtypes.bfloat16).astype(np.float64), axis, -1)
    blocks = v.reshape(v.shape[:-1] + (-1, 32))
    amax = np.abs(blocks).max(-1, keepdims=True)
    byte = np.maximum(np.where(amax > 0, np.frexp(amax)[1] - 1 + 127, 0) - down, 1)
    scale = np.exp2(byte - 127.0)
    codes = (blocks / scale).astype(np.float32).astype(dtype).astype(np.float64)
    return np.moveaxis((codes * scale).reshape(v.shape), -1, axis)


WIDE = False


def mx_kscale(k):
    if not WIDE:
        return np.ones(k)
    levels = np.array([18, -18])
    if k % 512:
        return np.exp2(np.random.permutation(np.resize(levels, k // 32))).repeat(32)
    a = np.empty((k // 512, 16))
    for p in range(k // 512):
        a[p, :8] = np.random.permutation(np.resize(levels, 8))
        for g in range(8):
            far = levels[np.abs(levels - a[p, g]) >= 10]
            a[p, g + 8] = far[np.random.randint(len(far))]
    return np.exp2(a.ravel()).repeat(32)


BF16 = ml_dtypes.bfloat16


def bf(x):
    return np.asarray(x, np.float32).astype(BF16)


def f64(x):
    return np.asarray(x).astype(np.float64)


B, T, E, H, DK = 1, 512, 1024, 4, 256
DV = 2 * DK
F = H * DV
EPS = 1e-5


def setup_inputs():
    s = mx_kscale(T)[:, None]
    u = mx_kscale(E)
    v = mx_kscale(F)
    o = bf(np.random.standard_normal((B, T, H, DV)) * 5.0 * np.exp(0.5 * np.random.standard_normal((B, T, H, 1))))
    x0 = bf(np.random.standard_normal((B, T, E)))
    wg0 = bf(np.random.standard_normal((E, F)) / np.sqrt(E))
    gn = bf(1.0 + 0.1 * np.random.standard_normal(DV))
    wo0 = bf(np.random.standard_normal((F, E)) / np.sqrt(F))
    g = bf(np.random.standard_normal((B, T, E)) * np.exp2(np.random.randint(-6, 1, (B, T, 1))) / s * u)
    of = f64(o)
    rstd = 1.0 / np.sqrt(np.mean(of * of, axis=-1) + EPS)
    return {"o_ret": o,
            "x": bf(f64(x0) * s),
            "Wg": bf(f64(wg0) / v),
            "gn_weight": gn,
            "Wo": bf(f64(wo0) * v[:, None] / u),
            "rstd": np.asarray(rstd, np.float32),
            "grad_out": g}


def reference(o_ret, x, Wg, gn_weight, Wo, rstd, grad_out):
    on = (f64(o_ret) * f64(rstd)[..., None] * f64(gn_weight)).reshape(B * T, F)
    go = f64(grad_out).reshape(B * T, E)
    xf = f64(x).reshape(B * T, E)
    dh = mxq(go, 1, "e5m2") @ mxq(f64(Wo), 1, "e4m3").T
    dg = dh * on
    dx = mxq(dg, 1, "e5m2") @ mxq(f64(Wg), 1, "e4m3").T
    dwg = mxq(xf, 0, "e4m3").T @ mxq(dg, 0, "e5m2")
    return dx.reshape(B, T, E), dwg

@@ -1,0 +1,288 @@
+from contextlib import ExitStack
+
+import concourse.mybir as mybir
+from concourse.masks import make_identity
+
+T, E, H, DV = 512, 1024, 4, 512
+F = H * DV
+FLOPS = 3 * 2 * T * E * F
+
+F32 = mybir.dt.float32
+BF16 = mybir.dt.bfloat16
+U32 = mybir.dt.uint32
+U8 = mybir.dt.uint8
+E4M3 = mybir.dt.float8_e4m3fn_x4
+E5M2 = mybir.dt.float8_e5m2_x4
+MULT = mybir.AluOpType.mult
+
+P = 128
+N = 512
+BANKS = 8
+
+
+def tile_multiscaleretention_pc_v_kernel(tc, o_ret, x, Wg, gn_weight, Wo, rstd, grad_out, out_0, out_1):
+    nc = tc.nc
+    o_v = o_ret.rearrange("b (p j) h d -> p (b j) h d", j=4)
+    x_v = x.rearrange("b (p j) e -> p (b j) e", j=4)
+    go_v = grad_out.rearrange("b (p j) e -> p (b j) e", j=4)
+    rstd_v = rstd.rearrange("b (p j) h -> p (b j h)", j=4)
+    gn_v = gn_weight.rearrange("(p c) -> p c", c=4)
+    wo_v = Wo.rearrange("(h p c) e -> p h c e", p=P, c=4)
+    wg_v = Wg.rearrange("(i p) f -> p i f", p=P)
+    out0_v = out_0.rearrange("b (p j) e -> p (b j) e", j=4)
+    out1_v = out_1.rearrange("(i p) f -> p i f", p=P)
+
+    with ExitStack() as ctx:
+        keep = ctx.enter_context(tc.tile_pool(name="keep", bufs=1))
+        flow = ctx.enter_context(tc.tile_pool(name="flow", bufs=2))
+        psum = ctx.enter_context(tc.psum_pool(name="psum", bufs=1))
+        ctx.enter_context(tc.manual_schedule())
+
+        banks_taken = []
+
+        def new_bank():
+            n = len(banks_taken)
+            banks_taken.append(n)
+            return psum.tile([P, N], F32, name="bank", tag="bank%d" % (n % BANKS))
+
+        def load(src, shape):
+            raw = flow.tile(shape, BF16, name="raw", tag="raw", bufs=16, align_bytes=64)
+            nc.sync.dma_start(out=raw[:], in_=src)
+            return raw
+
+        def load_wo(h):
+            return [load(wo_v[:, h, 2 * a : 2 * a + 2, :], [P, 2, E]) for a in range(2)]
+
+        def load_wg(q):
+            ec, hp = divmod(q, 2)
+            return [load(wg_v[:, 4 * ec + 2 * a : 4 * ec + 2 * a + 2, 1024 * hp : 1024 * (hp + 1)], [P, 2, 1024]) for a in range(2)]
+
+        def load_o(h):
+            return load(o_v[:, :, h, :], [P, 4, DV])
+
+        def new_stage():
+            return flow.tile([P, 4 * N], BF16, name="stage", tag="stage", bufs=8, align_bytes=64)
+
+        def mx_tiles(pool, name, width, bufs):
+            codes = pool.tile([P, width], U32, name=name + "_c", tag=name + "_c", bufs=bufs, align_bytes=64)
+            scales = pool.tile([P, width], U8, name=name + "_s", tag=name + "_s", bufs=bufs, align_bytes=64)
+            return codes, scales
+
+        def quantize(stage_ap, mx, cols, fmt):
+            nc.vector.quantize_mx(out=mx[0][:, cols].bitcast(fmt), scales=mx[1][:, cols], in_=stage_ap)
+
+        def mm(bank, lhs, lhs_cols, lhs_fmt, rhs, rhs_fmt, start, stop):
+            nc.tensor.matmul_mx(
+                out=bank[:],
+                lhsT=lhs[0][:, lhs_cols].bitcast(lhs_fmt),
+                lhsT_scale=lhs[1][:, lhs_cols],
+                rhs=rhs[0][:].bitcast(rhs_fmt),
+                rhs_scale=rhs[1][:],
+                start=start,
+                stop=stop,
+            )
+
+        def turn_pair(raw, g, stage, a, rows_inner):
+            words = raw[:].rearrange("p s k -> p (s k)").bitcast(F32)
+            bank = new_bank()
+            for s in range(2):
+                for u in range(2):
+                    lo = 512 * s + 256 * g
+                    nc.tensor.transpose(bank[:, P * (2 * s + u) : P * (2 * s + u + 1)], words[:, lo + u : lo + 256 : 2], ident[:])
+            dst = stage[:].bitcast(F32)[:, N * a : N * (a + 1)]
+            if rows_inner:
+                nc.scalar.copy(out=dst.rearrange("p (s r u) -> p s r u", s=2, u=2), in_=bank[:].rearrange("p (s u r) -> p s r u", s=2, u=2))
+            else:
+                nc.scalar.copy(out=dst.rearrange("p (r s u) -> p r s u", s=2, u=2), in_=bank[:].rearrange("p (s u r) -> p r s u", s=2, u=2))
+
+        def turn_block(raws, rows_inner):
+            stages = []
+            for g in range(2):
+                stage = new_stage()
+                for a in range(2):
+                    turn_pair(raws[a], g, stage, a, rows_inner)
+                stages.append(stage)
+            return stages
+
+        def interleave(copy, src, stage):
+            copy(out=stage[:].rearrange("p (c i t) -> p c t i", i=4, t=4), in_=src.rearrange("p t (c i) -> p c t i", i=4))
+
+        def gate(o_raw, j):
+            og = flow.tile([P, N], F32, name="og", tag="og", bufs=6)
+            nc.vector.tensor_tensor(
+                out=og[:].rearrange("p (u m e) -> p u m e", u=2, e=2),
+                in0=o_raw[:, j, :].rearrange("p (m u e) -> p u m e", u=2, e=2),
+                in1=gn_row[:].rearrange("p (u m e) -> p u m e", u=2, e=2),
+                op=MULT,
+            )
+            return og
+
+        def dh_tile(h, j):
+            bank = new_bank()
+            for g in range(2):
+                mm(bank, go_mx[g], slice(P * j, P * (j + 1)), E5M2, wo_mx[h][g], E4M3, g == 0, g == 1)
+            nc.vector.scalar_tensor_tensor(
+                out=dg[h][:, j, :], in0=bank[:], scalar=rstd_sb[:, 4 * j + h : 4 * j + h + 1], in1=ogs[h][j][:], op0=MULT, op1=MULT
+            )
+
+        def turn_dg(h, a, stage):
+            words = dg[h][:].rearrange("p j n -> p (j n)").bitcast(F32)
+            bank = new_bank()
+            for b in range(4):
+                nc.tensor.transpose(bank[:, P * b : P * (b + 1)], words[:, N * a + P * b : N * a + P * (b + 1)], ident[:])
+            dst = stage[:].bitcast(F32)[:, N * a : N * (a + 1)]
+            nc.scalar.copy(out=dst.rearrange("p (s r u) -> p s r u", s=2, u=2), in_=bank[:].rearrange("p (s u r) -> p s r u", s=2, u=2))
+
+        def new_result():
+            return flow.tile([P, 2, N], F32, name="result", tag="result", bufs=10)
+
+        def out1_tile(h, i, result, copy):
+            bank = new_bank()
+            mm(bank, x_mx, slice(P * i, P * (i + 1)), E4M3, dgt_mx[h], E5M2, True, True)
+            copy(out=result[:, i % 2, :].rearrange("p (m u e) -> p m u e", u=2, e=2), in_=bank[:].rearrange("p (u m e) -> p m u e", u=2, e=2))
+            if i % 2 == 1:
+                nc.sync.dma_start(out=out1_v[:, i - 1 : i + 1, N * h : N * (h + 1)], in_=result[:])
+
+        def out0_pass(bank, ec, j, h):
+            mm(bank, dgf_mx[h], slice(P * j, P * (j + 1)), E5M2, wg_mx[ec][h], E4M3, h == 0, h == H - 1)
+
+        def out0_store(bank, ec, j, result, copy):
+            copy(out=result[:, j % 2, :], in_=bank[:])
+            if j % 2 == 1:
+                nc.sync.dma_start(out=out0_v[:, j - 1 : j + 1, N * ec : N * (ec + 1)], in_=result[:])
+
+        gn_col = keep.tile([P, 4], BF16, name="gn_col")
+        nc.sync.dma_start(out=gn_col[:], in_=gn_v)
+        wo_raw, wg_raw, o_raw = {}, {}, {}
+        wo0_a = load(wo_v[:, 0, 0:2, :], [P, 2, E])
+        go_a = load(go_v[:, 0:2, :], [P, 2, E])
+        wo0_b = load(wo_v[:, 0, 2:4, :], [P, 2, E])
+        go_b = load(go_v[:, 2:4, :], [P, 2, E])
+        rstd_sb = keep.tile([P, 16], F32, name="rstd_sb")
+        nc.sync.dma_start(out=rstd_sb[:], in_=rstd_v)
+        o_raw[0] = load_o(0)
+        wo_raw[1] = load_wo(1)
+        x_raw = keep.tile([P, 4, E], BF16, name="x_raw", align_bytes=64)
+        nc.sync.dma_start(out=x_raw[:], in_=x_v)
+        wg_raw[0] = load_wg(0)
+        o_raw[1] = load_o(1)
+
+        ident = keep.tile([P, P], F32, name="ident")
+        make_identity(nc, ident[:])
+
+        gn_f32 = keep.tile([P, 4], F32, name="gn_f32")
+        nc.scalar.copy(out=gn_f32[:], in_=gn_col[:])
+        gn_row = keep.tile([P, N], F32, name="gn_row")
+        bank = new_bank()
+        for c in range(4):
+            nc.tensor.transpose(bank[:, P * c : P * (c + 1)], gn_f32[:, c : c + 1].to_broadcast([P, P]), ident[:])
+        nc.scalar.copy(out=gn_row[:].rearrange("p (u m e) -> p u m e", u=2, e=2), in_=bank[:].rearrange("p (u e m) -> p u m e", u=2, e=2))
+
+        go_mx = [mx_tiles(keep, "go%d" % g, N, 1) for g in range(2)]
+        x_mx = mx_tiles(keep, "x", E, 1)
+        wg_mx = [[mx_tiles(keep, "wg%d_%d" % (ec, h), N, 1) for h in range(H)] for ec in range(2)]
+        dgf_mx = [mx_tiles(keep, "dgf%d" % h, N, 1) for h in range(H)]
+        wo_mx, dgt_mx, dg, ogs = {}, {}, {}, {}
+        whole = slice(0, N)
+
+        def quantize_wo(h, g, stage):
+            mx = mx_tiles(flow, "wo", N, 4)
+            wo_mx.setdefault(h, []).append(mx)
+            quantize(stage[:], mx, whole, E4M3)
+
+        def quantize_wg(q, g, stage):
+            ec, hp = divmod(q, 2)
+            quantize(stage[:], wg_mx[ec][2 * hp + g], whole, E4M3)
+
+        wo_st = [new_stage() for g in range(2)]
+        go_st = [new_stage() for g in range(2)]
+        for a, (wo_half, go_half) in enumerate(((wo0_a, go_a), (wo0_b, go_b))):
+            for g in range(2):
+                turn_pair(wo_half, g, wo_st[g], a, False)
+            if a == 1:
+                for g in range(2):
+                    quantize_wo(0, g, wo_st[g])
+            for g in range(2):
+                turn_pair(go_half, g, go_st[g], a, True)
+            if a == 1:
+                ogs[0] = [gate(o_raw[0], j) for j in range(2)]
+            for g in range(2):
+                quantize(go_st[g][:, 1024 * a : 1024 * (a + 1)], go_mx[g], slice(256 * a, 256 * (a + 1)), E5M2)
+        ogs[0].extend(gate(o_raw[0], j) for j in range(2, 4))
+
+        wg_st = {}
+        for h in range(H):
+            if h + 2 < H:
+                wo_raw[h + 2] = load_wo(h + 2)
+            if h + 1 < H:
+                wg_raw[h + 1] = load_wg(h + 1)
+            if h + 2 < H:
+                o_raw[h + 2] = load_o(h + 2)
+            dg[h] = flow.tile([P, 4, N], BF16, name="dg", tag="dg", bufs=2, align_bytes=64)
+            dgf_st = new_stage()
+            for a in range(2):
+                results = [new_result() for k in range(2)] if h > 0 else []
+                dh_tile(h, 2 * a)
+                if h > 0:
+                    out1_tile(h - 1, 4 * a, results[0], nc.scalar.copy)
+                if a == 1 and h > 0:
+                    quantize_wg(h - 1, 1, wg_st[h - 1][1])
+                dh_tile(h, 2 * a + 1)
+                if h > 0:
+                    for i in range(4 * a + 1, 4 * a + 4):
+                        out1_tile(h - 1, i, results[(i % 4) // 2], nc.scalar.copy)
+                if a == 0:
+                    if h + 1 < H:
+                        ogs[h + 1] = [gate(o_raw[h + 1], j) for j in range(4)] if h > 0 else []
+                        wo_st = turn_block(wo_raw[h + 1], False)
+                    else:
+                        wg_st[h] = turn_block(wg_raw[h], True)
+                    turn_dg(h, 0, dgf_st)
+                    if h > 0:
+                        quantize_wg(h - 1, 0, wg_st[h - 1][0])
+                    if h + 1 < H:
+                        quantize_wo(h + 1, 0, wo_st[0])
+                    if h == 0:
+                        x_st = new_stage()
+                        interleave(nc.scalar.copy, x_raw[:, :, 0:N], x_st)
+                else:
+                    dgt_st = new_stage()
+                    interleave(nc.vector.tensor_copy, dg[h][:], dgt_st)
+                    if h + 1 < H:
+                        quantize_wo(h + 1, 1, wo_st[1])
+                        wg_st[h] = turn_block(wg_raw[h], True)
+                    else:
+                        quantize_wg(h, 0, wg_st[h][0])
+                    turn_dg(h, 1, dgf_st)
+                    dgt_mx[h] = mx_tiles(flow, "dgt", N, 2)
+                    quantize(dgt_st[:], dgt_mx[h], whole, E5M2)
+                    if h == 0:
+                        quantize(x_st[:], x_mx, slice(0, N), E4M3)
+                        ogs[1] = [gate(o_raw[1], j) for j in range(4)]
+                        x_st = new_stage()
+                        interleave(nc.vector.tensor_copy, x_raw[:, :, N:E], x_st)
+                    quantize(dgf_st[:], dgf_mx[h], whole, E5M2)
+                    if h == 0:
+                        quantize(x_st[:], x_mx, slice(N, E), E4M3)
+                    if h == H - 1:
+                        quantize_wg(h, 1, wg_st[h][1])
+
+        copies = (nc.scalar.copy, nc.vector.tensor_copy)
+        open_banks = [new_bank() for j in range(4)]
+        for j in range(4):
+            for h in range(H - 1):
+                out0_pass(open_banks[j], 0, j, h)
+        results = [new_result() for k in range(2)]
+        for i in range(4):
+            out1_tile(H - 1, i, results[i // 2], copies[i % 2])
+        results = [new_result() for k in range(2)]
+        for j in range(4):
+            out0_pass(open_banks[j], 0, j, H - 1)
+            out0_store(open_banks[j], 0, j, results[j // 2], copies[j % 2])
+        results = [new_result() for k in range(4)]
+        for j in range(4):
+            out1_tile(H - 1, 4 + j, results[j // 2], copies[0])
+            bank = new_bank()
+            for h in range(H):
+                out0_pass(bank, 1, j, h)
+            out0_store(bank, 1, j, results[2 + j // 2], copies[1])

@@ -18,19 +18,24 @@ MULT = mybir.AluOpType.mult
 P = 128
 N = 512
 BANKS = 8
+TILES = 4
+STEPS = H * TILES
+GATE_LEAD = 2
+OUT1_LAG = 2
 
 
 def tile_multiscaleretention_pc_v_kernel(tc, o_ret, x, Wg, gn_weight, Wo, rstd, grad_out, out_0, out_1):
     nc = tc.nc
-    o_v = o_ret.rearrange("b (p j) h d -> p (b j) h d", j=4)
-    x_v = x.rearrange("b (p j) e -> p (b j) e", j=4)
-    go_v = grad_out.rearrange("b (p j) e -> p (b j) e", j=4)
-    rstd_v = rstd.rearrange("b (p j) h -> p (b j h)", j=4)
-    gn_v = gn_weight.rearrange("(p c) -> p c", c=4)
-    wo_v = Wo.rearrange("(h p c) e -> p h c e", p=P, c=4)
-    wg_v = Wg.rearrange("(i p) f -> p i f", p=P)
-    out0_v = out_0.rearrange("b (p j) e -> p (b j) e", j=4)
-    out1_v = out_1.rearrange("(i p) f -> p i f", p=P)
+    o_hbm = o_ret.rearrange("b (p j) h d -> p (b j) h d", j=TILES)
+    x_hbm = x.rearrange("b (p j) e -> p (b j) e", j=TILES)
+    go_hbm = grad_out.rearrange("b (p j) e -> p (b j) e", j=TILES)
+    rstd_hbm = rstd.rearrange("b (p j) h -> p (b j h)", j=TILES)
+    out0_hbm = out_0.rearrange("b (p j) e -> p (b j) e", j=TILES)
+    gn_hbm = gn_weight.rearrange("(p c) -> p c", c=4)
+    wo_hbm = Wo.rearrange("(h p c) e -> p h c e", p=P, c=4)
+    wg_hbm = Wg.rearrange("(i p) f -> p i f", p=P)
+    out1_hbm = out_1.rearrange("(i p) f -> p i f", p=P)
+    on_scalar, on_vector = nc.scalar.copy, nc.vector.tensor_copy
 
     with ExitStack() as ctx:
         keep = ctx.enter_context(tc.tile_pool(name="keep", bufs=1))
@@ -41,131 +46,147 @@ def tile_multiscaleretention_pc_v_kernel(tc, o_ret, x, Wg, gn_weight, Wo, rstd, 
         banks_taken = []
 
         def new_bank():
-            n = len(banks_taken)
-            banks_taken.append(n)
-            return psum.tile([P, N], F32, name="bank", tag="bank%d" % (n % BANKS))
+            tag = "bank%d" % (len(banks_taken) % BANKS)
+            banks_taken.append(tag)
+            return psum.tile([P, N], F32, name="bank", tag=tag)
 
-        def load(src, shape):
-            raw = flow.tile(shape, BF16, name="raw", tag="raw", bufs=16, align_bytes=64)
+        def new_stage():
+            return flow.tile([P, 4 * N], BF16, name="stage", tag="stage", bufs=9, align_bytes=64)
+
+        def new_result():
+            return flow.tile([P, 2, N], F32, name="result", tag="result", bufs=9)
+
+        def new_mx(pool, name, width, bufs):
+            codes = pool.tile([P, width], U32, name=name + "_codes", tag=name + "_codes", bufs=bufs, align_bytes=64)
+            scales = pool.tile([P, width], U8, name=name + "_scales", tag=name + "_scales", bufs=bufs, align_bytes=64)
+            return codes, scales
+
+        def load(src):
+            raw = flow.tile(list(src.shape), BF16, name="raw", tag="raw", bufs=16, align_bytes=64)
             nc.sync.dma_start(out=raw[:], in_=src)
             return raw
 
         def load_wo(h):
-            return [load(wo_v[:, h, 2 * a : 2 * a + 2, :], [P, 2, E]) for a in range(2)]
+            return [load(wo_hbm[:, h, 2 * a : 2 * a + 2, :]) for a in range(2)]
 
         def load_wg(q):
-            ec, hp = divmod(q, 2)
-            return [load(wg_v[:, 4 * ec + 2 * a : 4 * ec + 2 * a + 2, 1024 * hp : 1024 * (hp + 1)], [P, 2, 1024]) for a in range(2)]
+            rows, cols = 4 * (q // 2), 2 * N * (q % 2)
+            return [load(wg_hbm[:, rows + 2 * a : rows + 2 * a + 2, cols : cols + 2 * N]) for a in range(2)]
 
-        def load_o(h):
-            return load(o_v[:, :, h, :], [P, 4, DV])
+        def quantize(values, mx, cols, fmt):
+            nc.vector.quantize_mx(out=mx[0][:, cols].bitcast(fmt), scales=mx[1][:, cols], in_=values)
 
-        def new_stage():
-            return flow.tile([P, 4 * N], BF16, name="stage", tag="stage", bufs=8, align_bytes=64)
-
-        def mx_tiles(pool, name, width, bufs):
-            codes = pool.tile([P, width], U32, name=name + "_c", tag=name + "_c", bufs=bufs, align_bytes=64)
-            scales = pool.tile([P, width], U8, name=name + "_s", tag=name + "_s", bufs=bufs, align_bytes=64)
-            return codes, scales
-
-        def quantize(stage_ap, mx, cols, fmt):
-            nc.vector.quantize_mx(out=mx[0][:, cols].bitcast(fmt), scales=mx[1][:, cols], in_=stage_ap)
-
-        def mm(bank, lhs, lhs_cols, lhs_fmt, rhs, rhs_fmt, start, stop):
+        def product(bank, lhs, block, lhs_fmt, rhs, rhs_fmt, start, stop):
+            cols = slice(P * block, P * (block + 1))
             nc.tensor.matmul_mx(
                 out=bank[:],
-                lhsT=lhs[0][:, lhs_cols].bitcast(lhs_fmt),
-                lhsT_scale=lhs[1][:, lhs_cols],
+                lhsT=lhs[0][:, cols].bitcast(lhs_fmt),
+                lhsT_scale=lhs[1][:, cols],
                 rhs=rhs[0][:].bitcast(rhs_fmt),
                 rhs_scale=rhs[1][:],
                 start=start,
                 stop=stop,
             )
 
-        def turn_pair(raw, g, stage, a, rows_inner):
+        def bank_to_stage(bank, stage, a, order, copy):
+            dst = stage[:].bitcast(F32)[:, N * a : N * (a + 1)]
+            copy(
+                out=dst.rearrange("p (%s u) -> p %s u" % (order, order), s=2, u=2),
+                in_=bank[:].rearrange("p (s u r) -> p %s u" % order, s=2, u=2),
+            )
+
+        def turn_rows(raw, g, stage, a, order, copy):
             words = raw[:].rearrange("p s k -> p (s k)").bitcast(F32)
             bank = new_bank()
             for s in range(2):
                 for u in range(2):
-                    lo = 512 * s + 256 * g
-                    nc.tensor.transpose(bank[:, P * (2 * s + u) : P * (2 * s + u + 1)], words[:, lo + u : lo + 256 : 2], ident[:])
-            dst = stage[:].bitcast(F32)[:, N * a : N * (a + 1)]
-            if rows_inner:
-                nc.scalar.copy(out=dst.rearrange("p (s r u) -> p s r u", s=2, u=2), in_=bank[:].rearrange("p (s u r) -> p s r u", s=2, u=2))
+                    first = N * s + 2 * P * g
+                    block = slice(P * (2 * s + u), P * (2 * s + u + 1))
+                    nc.tensor.transpose(bank[:, block], words[:, first + u : first + 2 * P : 2], ident[:])
+            bank_to_stage(bank, stage, a, order, copy)
+
+        def turn_weight(kind, q, g):
+            stage = new_stage()
+            for a in range(2):
+                if kind == "wo":
+                    turn_rows(wo_raw[q][a], g, stage, a, "r s", on_scalar)
+                else:
+                    turn_rows(wg_raw[q][a], g, stage, a, "s r", on_scalar)
+            return kind, q, g, stage
+
+        def quantize_weight(kind, q, g, stage):
+            if kind == "wo":
+                mx = wo_mx[q, g] = new_mx(flow, "wo", N, 4)
             else:
-                nc.scalar.copy(out=dst.rearrange("p (r s u) -> p r s u", s=2, u=2), in_=bank[:].rearrange("p (s u r) -> p r s u", s=2, u=2))
+                mx = wg_mx[q // 2][2 * (q % 2) + g]
+            quantize(stage[:], mx, whole, E4M3)
 
-        def turn_block(raws, rows_inner):
-            stages = []
-            for g in range(2):
-                stage = new_stage()
-                for a in range(2):
-                    turn_pair(raws[a], g, stage, a, rows_inner)
-                stages.append(stage)
-            return stages
-
-        def interleave(copy, src, stage):
-            copy(out=stage[:].rearrange("p (c i t) -> p c t i", i=4, t=4), in_=src.rearrange("p t (c i) -> p c t i", i=4))
-
-        def gate(o_raw, j):
-            og = flow.tile([P, N], F32, name="og", tag="og", bufs=6)
-            nc.vector.tensor_tensor(
-                out=og[:].rearrange("p (u m e) -> p u m e", u=2, e=2),
-                in0=o_raw[:, j, :].rearrange("p (m u e) -> p u m e", u=2, e=2),
-                in1=gn_row[:].rearrange("p (u m e) -> p u m e", u=2, e=2),
-                op=MULT,
-            )
-            return og
-
-        def dh_tile(h, j):
-            bank = new_bank()
-            for g in range(2):
-                mm(bank, go_mx[g], slice(P * j, P * (j + 1)), E5M2, wo_mx[h][g], E4M3, g == 0, g == 1)
-            nc.vector.scalar_tensor_tensor(
-                out=dg[h][:, j, :], in0=bank[:], scalar=rstd_sb[:, 4 * j + h : 4 * j + h + 1], in1=ogs[h][j][:], op0=MULT, op1=MULT
-            )
-
-        def turn_dg(h, a, stage):
+        def turn_dg(h, a):
             words = dg[h][:].rearrange("p j n -> p (j n)").bitcast(F32)
             bank = new_bank()
             for b in range(4):
                 nc.tensor.transpose(bank[:, P * b : P * (b + 1)], words[:, N * a + P * b : N * a + P * (b + 1)], ident[:])
-            dst = stage[:].bitcast(F32)[:, N * a : N * (a + 1)]
-            nc.scalar.copy(out=dst.rearrange("p (s r u) -> p s r u", s=2, u=2), in_=bank[:].rearrange("p (s u r) -> p s r u", s=2, u=2))
+            bank_to_stage(bank, dg_f_stage[h], a, "s r", on_scalar)
 
-        def new_result():
-            return flow.tile([P, 2, N], F32, name="result", tag="result", bufs=10)
+        def interleave(tiles, copy):
+            stage = new_stage()
+            copy(out=stage[:].rearrange("p (c i j) -> p c j i", i=4, j=TILES), in_=tiles.rearrange("p j (c i) -> p c j i", i=4))
+            return stage
 
-        def out1_tile(h, i, result, copy):
+        def make_gate(step):
+            h, j = divmod(step, TILES)
+            gate[step] = flow.tile([P, N], F32, name="gate", tag="gate", bufs=GATE_LEAD + 2)
+            nc.vector.tensor_tensor(
+                out=gate[step][:].rearrange("p (u m e) -> p u m e", u=2, e=2),
+                in0=o_raw[h][:, j, :].rearrange("p (m u e) -> p u m e", u=2, e=2),
+                in1=gn_row[:].rearrange("p (u m e) -> p u m e", u=2, e=2),
+                op=MULT,
+            )
+
+        def make_dg(step):
+            h, j = divmod(step, TILES)
             bank = new_bank()
-            mm(bank, x_mx, slice(P * i, P * (i + 1)), E4M3, dgt_mx[h], E5M2, True, True)
-            copy(out=result[:, i % 2, :].rearrange("p (m u e) -> p m u e", u=2, e=2), in_=bank[:].rearrange("p (u m e) -> p m u e", u=2, e=2))
-            if i % 2 == 1:
-                nc.sync.dma_start(out=out1_v[:, i - 1 : i + 1, N * h : N * (h + 1)], in_=result[:])
+            for g in range(2):
+                product(bank, go_mx[g], j, E5M2, wo_mx[h, g], E4M3, g == 0, g == 1)
+            scale = rstd_sb[:, H * j + h : H * j + h + 1]
+            nc.vector.scalar_tensor_tensor(out=dg[h][:, j, :], in0=bank[:], scalar=scale, in1=gate[step][:], op0=MULT, op1=MULT)
 
-        def out0_pass(bank, ec, j, h):
-            mm(bank, dgf_mx[h], slice(P * j, P * (j + 1)), E5M2, wg_mx[ec][h], E4M3, h == 0, h == H - 1)
+        def quantize_dg_tokens(h):
+            dg_t_mx[h] = new_mx(flow, "dg_t", N, 2)
+            quantize(dg_t_stage[h][:], dg_t_mx[h], whole, E5M2)
 
-        def out0_store(bank, ec, j, result, copy):
+        def out1_pair(pair, copies):
+            h, k = divmod(pair, 4)
+            result = new_result()
+            for i in range(2):
+                bank = new_bank()
+                product(bank, x_mx, 2 * k + i, E4M3, dg_t_mx[h], E5M2, True, True)
+                copies[i](
+                    out=result[:, i, :].rearrange("p (m u e) -> p m u e", u=2, e=2),
+                    in_=bank[:].rearrange("p (u m e) -> p m u e", u=2, e=2),
+                )
+            nc.sync.dma_start(out=out1_hbm[:, 2 * k : 2 * k + 2, N * h : N * (h + 1)], in_=result[:])
+
+        def out0_tile(half, j, result, copy):
+            bank = new_bank()
+            for h in range(H):
+                product(bank, dg_f_mx[h], j, E5M2, wg_mx[half][h], E4M3, h == 0, h == H - 1)
             copy(out=result[:, j % 2, :], in_=bank[:])
-            if j % 2 == 1:
-                nc.sync.dma_start(out=out0_v[:, j - 1 : j + 1, N * ec : N * (ec + 1)], in_=result[:])
 
         gn_col = keep.tile([P, 4], BF16, name="gn_col")
-        nc.sync.dma_start(out=gn_col[:], in_=gn_v)
-        wo_raw, wg_raw, o_raw = {}, {}, {}
-        wo0_a = load(wo_v[:, 0, 0:2, :], [P, 2, E])
-        go_a = load(go_v[:, 0:2, :], [P, 2, E])
-        wo0_b = load(wo_v[:, 0, 2:4, :], [P, 2, E])
-        go_b = load(go_v[:, 2:4, :], [P, 2, E])
-        rstd_sb = keep.tile([P, 16], F32, name="rstd_sb")
-        nc.sync.dma_start(out=rstd_sb[:], in_=rstd_v)
-        o_raw[0] = load_o(0)
+        nc.sync.dma_start(out=gn_col[:], in_=gn_hbm)
+        wo_raw, wg_raw, o_raw, go_raw = {0: []}, {}, {}, []
+        for a in range(2):
+            wo_raw[0].append(load(wo_hbm[:, 0, 2 * a : 2 * a + 2, :]))
+            go_raw.append(load(go_hbm[:, 2 * a : 2 * a + 2, :]))
+        rstd_sb = keep.tile([P, TILES * H], F32, name="rstd_sb")
+        nc.sync.dma_start(out=rstd_sb[:], in_=rstd_hbm)
+        o_raw[0] = load(o_hbm[:, :, 0, :])
         wo_raw[1] = load_wo(1)
-        x_raw = keep.tile([P, 4, E], BF16, name="x_raw", align_bytes=64)
-        nc.sync.dma_start(out=x_raw[:], in_=x_v)
-        wg_raw[0] = load_wg(0)
-        o_raw[1] = load_o(1)
+        o_raw[1] = load(o_hbm[:, :, 1, :])
+        x_raw = keep.tile([P, TILES, E], BF16, name="x_raw", align_bytes=64)
+        nc.sync.dma_start(out=x_raw[:], in_=x_hbm)
+        wo_raw[2], wg_raw[0], o_raw[2] = load_wo(2), load_wg(0), load(o_hbm[:, :, 2, :])
 
         ident = keep.tile([P, P], F32, name="ident")
         make_identity(nc, ident[:])
@@ -173,116 +194,97 @@ def tile_multiscaleretention_pc_v_kernel(tc, o_ret, x, Wg, gn_weight, Wo, rstd, 
         gn_f32 = keep.tile([P, 4], F32, name="gn_f32")
         nc.scalar.copy(out=gn_f32[:], in_=gn_col[:])
         gn_row = keep.tile([P, N], F32, name="gn_row")
-        bank = new_bank()
+        gn_bank = new_bank()
         for c in range(4):
-            nc.tensor.transpose(bank[:, P * c : P * (c + 1)], gn_f32[:, c : c + 1].to_broadcast([P, P]), ident[:])
-        nc.scalar.copy(out=gn_row[:].rearrange("p (u m e) -> p u m e", u=2, e=2), in_=bank[:].rearrange("p (u e m) -> p u m e", u=2, e=2))
+            nc.tensor.transpose(gn_bank[:, P * c : P * (c + 1)], gn_f32[:, c : c + 1].to_broadcast([P, P]), ident[:])
+        nc.vector.tensor_copy(
+            out=gn_row[:].rearrange("p (u m e) -> p u m e", u=2, e=2),
+            in_=gn_bank[:].rearrange("p (u e m) -> p u m e", u=2, e=2),
+        )
 
-        go_mx = [mx_tiles(keep, "go%d" % g, N, 1) for g in range(2)]
-        x_mx = mx_tiles(keep, "x", E, 1)
-        wg_mx = [[mx_tiles(keep, "wg%d_%d" % (ec, h), N, 1) for h in range(H)] for ec in range(2)]
-        dgf_mx = [mx_tiles(keep, "dgf%d" % h, N, 1) for h in range(H)]
-        wo_mx, dgt_mx, dg, ogs = {}, {}, {}, {}
+        go_mx = [new_mx(keep, "go%d" % g, N, 1) for g in range(2)]
+        x_mx = new_mx(keep, "x", E, 1)
+        wg_mx = [[new_mx(keep, "wg%d_%d" % (half, h), N, 1) for h in range(H)] for half in range(2)]
+        dg_f_mx = [new_mx(keep, "dg_f%d" % h, N, 1) for h in range(H)]
+        wo_mx, dg_t_mx, dg, gate, dg_f_stage, dg_t_stage, x_stage = {}, {}, {}, {}, {}, {}, {}
         whole = slice(0, N)
 
-        def quantize_wo(h, g, stage):
-            mx = mx_tiles(flow, "wo", N, 4)
-            wo_mx.setdefault(h, []).append(mx)
-            quantize(stage[:], mx, whole, E4M3)
+        wo_stage = [new_stage() for g in range(2)]
+        go_stage = [new_stage() for g in range(2)]
 
-        def quantize_wg(q, g, stage):
-            ec, hp = divmod(q, 2)
-            quantize(stage[:], wg_mx[ec][2 * hp + g], whole, E4M3)
+        def quantize_go(a, g):
+            quantize(go_stage[g][:, 2 * N * a : 2 * N * (a + 1)], go_mx[g], slice(2 * P * a, 2 * P * (a + 1)), E5M2)
 
-        wo_st = [new_stage() for g in range(2)]
-        go_st = [new_stage() for g in range(2)]
-        for a, (wo_half, go_half) in enumerate(((wo0_a, go_a), (wo0_b, go_b))):
-            for g in range(2):
-                turn_pair(wo_half, g, wo_st[g], a, False)
-            if a == 1:
-                for g in range(2):
-                    quantize_wo(0, g, wo_st[g])
-            for g in range(2):
-                turn_pair(go_half, g, go_st[g], a, True)
-            if a == 1:
-                ogs[0] = [gate(o_raw[0], j) for j in range(2)]
-            for g in range(2):
-                quantize(go_st[g][:, 1024 * a : 1024 * (a + 1)], go_mx[g], slice(256 * a, 256 * (a + 1)), E5M2)
-        ogs[0].extend(gate(o_raw[0], j) for j in range(2, 4))
+        for g in range(2):
+            turn_rows(wo_raw[0][0], g, wo_stage[g], 0, "r s", (on_scalar, on_vector)[g])
+        for g in range(2):
+            turn_rows(go_raw[0], g, go_stage[g], 0, "s r", (on_scalar, on_vector)[g])
+        for g in range(2):
+            turn_rows(wo_raw[0][1], g, wo_stage[g], 1, "r s", on_scalar)
+            quantize_go(0, g)
+        for g in range(2):
+            turn_rows(go_raw[1], g, go_stage[g], 1, "s r", on_scalar)
+            quantize_weight("wo", 0, g, wo_stage[g])
+        for step in range(GATE_LEAD):
+            make_gate(step)
+        wo_raw[3], wg_raw[1], o_raw[3], wg_raw[2] = load_wo(3), load_wg(1), load(o_hbm[:, :, 3, :]), load_wg(2)
 
-        wg_st = {}
-        for h in range(H):
-            if h + 2 < H:
-                wo_raw[h + 2] = load_wo(h + 2)
-            if h + 1 < H:
-                wg_raw[h + 1] = load_wg(h + 1)
-            if h + 2 < H:
-                o_raw[h + 2] = load_o(h + 2)
-            dg[h] = flow.tile([P, 4, N], BF16, name="dg", tag="dg", bufs=2, align_bytes=64)
-            dgf_st = new_stage()
-            for a in range(2):
-                results = [new_result() for k in range(2)] if h > 0 else []
-                dh_tile(h, 2 * a)
-                if h > 0:
-                    out1_tile(h - 1, 4 * a, results[0], nc.scalar.copy)
-                if a == 1 and h > 0:
-                    quantize_wg(h - 1, 1, wg_st[h - 1][1])
-                dh_tile(h, 2 * a + 1)
-                if h > 0:
-                    for i in range(4 * a + 1, 4 * a + 4):
-                        out1_tile(h - 1, i, results[(i % 4) // 2], nc.scalar.copy)
-                if a == 0:
-                    if h + 1 < H:
-                        ogs[h + 1] = [gate(o_raw[h + 1], j) for j in range(4)] if h > 0 else []
-                        wo_st = turn_block(wo_raw[h + 1], False)
-                    else:
-                        wg_st[h] = turn_block(wg_raw[h], True)
-                    turn_dg(h, 0, dgf_st)
-                    if h > 0:
-                        quantize_wg(h - 1, 0, wg_st[h - 1][0])
-                    if h + 1 < H:
-                        quantize_wo(h + 1, 0, wo_st[0])
-                    if h == 0:
-                        x_st = new_stage()
-                        interleave(nc.scalar.copy, x_raw[:, :, 0:N], x_st)
-                else:
-                    dgt_st = new_stage()
-                    interleave(nc.vector.tensor_copy, dg[h][:], dgt_st)
-                    if h + 1 < H:
-                        quantize_wo(h + 1, 1, wo_st[1])
-                        wg_st[h] = turn_block(wg_raw[h], True)
-                    else:
-                        quantize_wg(h, 0, wg_st[h][0])
-                    turn_dg(h, 1, dgf_st)
-                    dgt_mx[h] = mx_tiles(flow, "dgt", N, 2)
-                    quantize(dgt_st[:], dgt_mx[h], whole, E5M2)
-                    if h == 0:
-                        quantize(x_st[:], x_mx, slice(0, N), E4M3)
-                        ogs[1] = [gate(o_raw[1], j) for j in range(4)]
-                        x_st = new_stage()
-                        interleave(nc.vector.tensor_copy, x_raw[:, :, N:E], x_st)
-                    quantize(dgf_st[:], dgf_mx[h], whole, E5M2)
-                    if h == 0:
-                        quantize(x_st[:], x_mx, slice(N, E), E4M3)
-                    if h == H - 1:
-                        quantize_wg(h, 1, wg_st[h][1])
+        def weight_of(step):
+            h, j = divmod(step, TILES)
+            if j < 2:
+                return ("wo", h + 1, j) if h + 1 < H else ("wg", 2, j)
+            return ("wg", h - 1, j - 2) if 0 < h < H - 1 else None
 
-        copies = (nc.scalar.copy, nc.vector.tensor_copy)
-        open_banks = [new_bank() for j in range(4)]
-        for j in range(4):
-            for h in range(H - 1):
-                out0_pass(open_banks[j], 0, j, h)
+        turned = None
+        pairs_done = 0
+        for step in range(STEPS):
+            h, j = divmod(step, TILES)
+            if step == 2:
+                wg_raw[3] = load_wg(3)
+            if j == 0:
+                dg[h] = flow.tile([P, TILES, N], BF16, name="dg", tag="dg", bufs=2, align_bytes=64)
+            make_dg(step)
+            if step < 2:
+                quantize_go(1, step)
+            if j == 0 and h > 0:
+                quantize_dg_tokens(h - 1)
+            if step - 4 in x_stage:
+                quantize(x_stage[step - 4][:], x_mx, slice(N * (step - 4), N * (step - 3)), E4M3)
+            if turned:
+                quantize_weight(*turned)
+            if step + GATE_LEAD < STEPS:
+                make_gate(step + GATE_LEAD)
+            if j == 2 and h > 0:
+                quantize(dg_f_stage[h - 1][:], dg_f_mx[h - 1], whole, E5M2)
+            due = step - TILES - OUT1_LAG + 1 + (1 if step >= STEPS - 2 else 0)
+            for pair in range(pairs_done, due):
+                out1_pair(pair, (on_scalar, on_scalar))
+            pairs_done = max(pairs_done, due)
+            if j == TILES - 1:
+                dg_t_stage[h] = interleave(dg[h][:], on_vector)
+            turned = turn_weight(*weight_of(step)) if weight_of(step) else None
+            if j == 1:
+                dg_f_stage[h] = new_stage()
+            if j % 2 == 1:
+                turn_dg(h, j // 2)
+            if step in (2, 3):
+                x_stage[step - 2] = interleave(x_raw[:, :, N * (step - 2) : N * (step - 1)], on_scalar)
+
+        last = H - 1
+        turned_late = [turn_weight("wg", last, g) for g in range(2)]
+        quantize_dg_tokens(last)
+        quantize(dg_f_stage[last][:], dg_f_mx[last], whole, E5M2)
+        for pair in range(pairs_done, TILES * last):
+            out1_pair(pair, (on_scalar, on_scalar))
         results = [new_result() for k in range(2)]
-        for i in range(4):
-            out1_tile(H - 1, i, results[i // 2], copies[i % 2])
+        for j in range(TILES):
+            out1_pair(TILES * last + j, (on_scalar, on_vector if j < 2 else on_scalar))
+            if j >= 2:
+                quantize_weight(*turned_late[j - 2])
+            out0_tile(0, j, results[j // 2], on_vector)
+            if j % 2 == 1:
+                nc.sync.dma_start(out=out0_hbm[:, j - 1 : j + 1, 0:N], in_=results[j // 2][:])
         results = [new_result() for k in range(2)]
-        for j in range(4):
-            out0_pass(open_banks[j], 0, j, H - 1)
-            out0_store(open_banks[j], 0, j, results[j // 2], copies[j % 2])
-        results = [new_result() for k in range(4)]
-        for j in range(4):
-            out1_tile(H - 1, 4 + j, results[j // 2], copies[0])
-            bank = new_bank()
-            for h in range(H):
-                out0_pass(bank, 1, j, h)
-            out0_store(bank, 1, j, results[2 + j // 2], copies[1])
+        for j in range(TILES):
+            out0_tile(1, j, results[j // 2], (on_vector, on_scalar)[j % 2])
+            nc.sync.dma_start(out=out0_hbm[:, j, N:E], in_=results[j // 2][:, j % 2, :])

@@ -21,7 +21,14 @@ BANKS = 8
 TILES = 4
 STEPS = H * TILES
 GATE_LEAD = 2
-OUT1_LAG = 2
+OUT1_START = 6
+X_COPY_STEPS = (1, 3)
+X_QUANT_STEPS = (4, 5)
+EARLY_TILES = 2
+
+RAW_BUFS = 16
+STAGE_BUFS = 11
+RESULT_BUFS = 9
 
 
 def tile_multiscaleretention_pc_v_kernel(tc, o_ret, x, Wg, gn_weight, Wo, rstd, grad_out, out_0, out_1):
@@ -36,6 +43,8 @@ def tile_multiscaleretention_pc_v_kernel(tc, o_ret, x, Wg, gn_weight, Wo, rstd, 
     wg_hbm = Wg.rearrange("(i p) f -> p i f", p=P)
     out1_hbm = out_1.rearrange("(i p) f -> p i f", p=P)
     on_scalar, on_vector = nc.scalar.copy, nc.vector.tensor_copy
+    whole = slice(0, N)
+    last = H - 1
 
     with ExitStack() as ctx:
         keep = ctx.enter_context(tc.tile_pool(name="keep", bufs=1))
@@ -51,10 +60,10 @@ def tile_multiscaleretention_pc_v_kernel(tc, o_ret, x, Wg, gn_weight, Wo, rstd, 
             return psum.tile([P, N], F32, name="bank", tag=tag)
 
         def new_stage():
-            return flow.tile([P, 4 * N], BF16, name="stage", tag="stage", bufs=9, align_bytes=64)
+            return flow.tile([P, 4 * N], BF16, name="stage", tag="stage", bufs=STAGE_BUFS, align_bytes=64)
 
         def new_result():
-            return flow.tile([P, 2, N], F32, name="result", tag="result", bufs=9)
+            return flow.tile([P, 2, N], F32, name="result", tag="result", bufs=RESULT_BUFS)
 
         def new_mx(pool, name, width, bufs):
             codes = pool.tile([P, width], U32, name=name + "_codes", tag=name + "_codes", bufs=bufs, align_bytes=64)
@@ -62,7 +71,7 @@ def tile_multiscaleretention_pc_v_kernel(tc, o_ret, x, Wg, gn_weight, Wo, rstd, 
             return codes, scales
 
         def load(src):
-            raw = flow.tile(list(src.shape), BF16, name="raw", tag="raw", bufs=16, align_bytes=64)
+            raw = flow.tile(list(src.shape), BF16, name="raw", tag="raw", bufs=RAW_BUFS, align_bytes=64)
             nc.sync.dma_start(out=raw[:], in_=src)
             return raw
 
@@ -89,9 +98,9 @@ def tile_multiscaleretention_pc_v_kernel(tc, o_ret, x, Wg, gn_weight, Wo, rstd, 
             )
 
         def bank_to_stage(bank, stage, a, order, copy):
-            dst = stage[:].bitcast(F32)[:, N * a : N * (a + 1)]
+            half_stage = stage[:].bitcast(F32)[:, N * a : N * (a + 1)]
             copy(
-                out=dst.rearrange("p (%s u) -> p %s u" % (order, order), s=2, u=2),
+                out=half_stage.rearrange("p (%s u) -> p %s u" % (order, order), s=2, u=2),
                 in_=bank[:].rearrange("p (s u r) -> p %s u" % order, s=2, u=2),
             )
 
@@ -112,7 +121,7 @@ def tile_multiscaleretention_pc_v_kernel(tc, o_ret, x, Wg, gn_weight, Wo, rstd, 
                     turn_rows(wo_raw[q][a], g, stage, a, "r s", on_scalar)
                 else:
                     turn_rows(wg_raw[q][a], g, stage, a, "s r", on_scalar)
-            return kind, q, g, stage
+            turned.append((kind, q, g, stage))
 
         def quantize_weight(kind, q, g, stage):
             if kind == "wo":
@@ -155,23 +164,21 @@ def tile_multiscaleretention_pc_v_kernel(tc, o_ret, x, Wg, gn_weight, Wo, rstd, 
             dg_t_mx[h] = new_mx(flow, "dg_t", N, 2)
             quantize(dg_t_stage[h][:], dg_t_mx[h], whole, E5M2)
 
-        def out1_pair(pair, copies):
+        def out1_pair(pair):
             h, k = divmod(pair, 4)
             result = new_result()
             for i in range(2):
                 bank = new_bank()
                 product(bank, x_mx, 2 * k + i, E4M3, dg_t_mx[h], E5M2, True, True)
-                copies[i](
+                on_scalar(
                     out=result[:, i, :].rearrange("p (m u e) -> p m u e", u=2, e=2),
                     in_=bank[:].rearrange("p (u m e) -> p m u e", u=2, e=2),
                 )
             nc.sync.dma_start(out=out1_hbm[:, 2 * k : 2 * k + 2, N * h : N * (h + 1)], in_=result[:])
 
-        def out0_tile(half, j, result, copy):
-            bank = new_bank()
-            for h in range(H):
-                product(bank, dg_f_mx[h], j, E5M2, wg_mx[half][h], E4M3, h == 0, h == H - 1)
-            copy(out=result[:, j % 2, :], in_=bank[:])
+        def out0_passes(bank, half, j, heads):
+            for h in heads:
+                product(bank, dg_f_mx[h], j, E5M2, wg_mx[half][h], E4M3, h == 0, h == last)
 
         gn_col = keep.tile([P, 4], BF16, name="gn_col")
         nc.sync.dma_start(out=gn_col[:], in_=gn_hbm)
@@ -186,7 +193,8 @@ def tile_multiscaleretention_pc_v_kernel(tc, o_ret, x, Wg, gn_weight, Wo, rstd, 
         o_raw[1] = load(o_hbm[:, :, 1, :])
         x_raw = keep.tile([P, TILES, E], BF16, name="x_raw", align_bytes=64)
         nc.sync.dma_start(out=x_raw[:], in_=x_hbm)
-        wo_raw[2], wg_raw[0], o_raw[2] = load_wo(2), load_wg(0), load(o_hbm[:, :, 2, :])
+        wo_raw[2] = load_wo(2)
+        wg_raw[0] = load_wg(0)
 
         ident = keep.tile([P, P], F32, name="ident")
         make_identity(nc, ident[:])
@@ -207,7 +215,6 @@ def tile_multiscaleretention_pc_v_kernel(tc, o_ret, x, Wg, gn_weight, Wo, rstd, 
         wg_mx = [[new_mx(keep, "wg%d_%d" % (half, h), N, 1) for h in range(H)] for half in range(2)]
         dg_f_mx = [new_mx(keep, "dg_f%d" % h, N, 1) for h in range(H)]
         wo_mx, dg_t_mx, dg, gate, dg_f_stage, dg_t_stage, x_stage = {}, {}, {}, {}, {}, {}, {}
-        whole = slice(0, N)
 
         wo_stage = [new_stage() for g in range(2)]
         go_stage = [new_stage() for g in range(2)]
@@ -227,20 +234,18 @@ def tile_multiscaleretention_pc_v_kernel(tc, o_ret, x, Wg, gn_weight, Wo, rstd, 
             quantize_weight("wo", 0, g, wo_stage[g])
         for step in range(GATE_LEAD):
             make_gate(step)
-        wo_raw[3], wg_raw[1], o_raw[3], wg_raw[2] = load_wo(3), load_wg(1), load(o_hbm[:, :, 3, :]), load_wg(2)
+        o_raw[2] = load(o_hbm[:, :, 2, :])
+        wo_raw[3] = load_wo(3)
+        wg_raw[1] = load_wg(1)
+        o_raw[3] = load(o_hbm[:, :, 3, :])
+        wg_raw[2] = load_wg(2)
 
-        def weight_of(step):
-            h, j = divmod(step, TILES)
-            if j < 2:
-                return ("wo", h + 1, j) if h + 1 < H else ("wg", 2, j)
-            return ("wg", h - 1, j - 2) if 0 < h < H - 1 else None
-
-        turned = None
-        pairs_done = 0
+        blocks = [("wo", 1), None, ("wo", 2), ("wg", 0), ("wo", 3), ("wg", 1), ("wg", 2), ("wg", 3)]
+        turned = []
         for step in range(STEPS):
             h, j = divmod(step, TILES)
-            if step == 2:
-                wg_raw[3] = load_wg(3)
+            if step == TILES:
+                wg_raw[last] = load_wg(last)
             if j == 0:
                 dg[h] = flow.tile([P, TILES, N], BF16, name="dg", tag="dg", bufs=2, align_bytes=64)
             make_dg(step)
@@ -248,43 +253,55 @@ def tile_multiscaleretention_pc_v_kernel(tc, o_ret, x, Wg, gn_weight, Wo, rstd, 
                 quantize_go(1, step)
             if j == 0 and h > 0:
                 quantize_dg_tokens(h - 1)
-            if step - 4 in x_stage:
-                quantize(x_stage[step - 4][:], x_mx, slice(N * (step - 4), N * (step - 3)), E4M3)
-            if turned:
-                quantize_weight(*turned)
+            if step in X_QUANT_STEPS:
+                half = X_QUANT_STEPS.index(step)
+                quantize(x_stage[half][:], x_mx, slice(N * half, N * (half + 1)), E4M3)
+            if turned and step < STEPS - 1:
+                quantize_weight(*turned.pop(0))
             if step + GATE_LEAD < STEPS:
                 make_gate(step + GATE_LEAD)
             if j == 2 and h > 0:
                 quantize(dg_f_stage[h - 1][:], dg_f_mx[h - 1], whole, E5M2)
-            due = step - TILES - OUT1_LAG + 1 + (1 if step >= STEPS - 2 else 0)
-            for pair in range(pairs_done, due):
-                out1_pair(pair, (on_scalar, on_scalar))
-            pairs_done = max(pairs_done, due)
+            if step >= OUT1_START:
+                out1_pair(step - OUT1_START)
             if j == TILES - 1:
                 dg_t_stage[h] = interleave(dg[h][:], on_vector)
-            turned = turn_weight(*weight_of(step)) if weight_of(step) else None
-            if j == 1:
+            if blocks[step // 2]:
+                turn_weight(*blocks[step // 2], step % 2)
+            if j == 2:
                 dg_f_stage[h] = new_stage()
-            if j % 2 == 1:
-                turn_dg(h, j // 2)
-            if step in (2, 3):
-                x_stage[step - 2] = interleave(x_raw[:, :, N * (step - 2) : N * (step - 1)], on_scalar)
+                turn_dg(h, 0)
+            if j == 0 and h > 0:
+                turn_dg(h - 1, 1)
+            if step in X_COPY_STEPS:
+                half = X_COPY_STEPS.index(step)
+                x_stage[half] = interleave(x_raw[:, :, N * half : N * (half + 1)], on_scalar)
 
-        last = H - 1
-        turned_late = [turn_weight("wg", last, g) for g in range(2)]
+        turn_dg(last, 1)
         quantize_dg_tokens(last)
         quantize(dg_f_stage[last][:], dg_f_mx[last], whole, E5M2)
-        for pair in range(pairs_done, TILES * last):
-            out1_pair(pair, (on_scalar, on_scalar))
+        for pair in range(STEPS - OUT1_START, TILES * last):
+            out1_pair(pair)
+        early_banks = [new_bank() for j in range(EARLY_TILES)]
+        for j in range(EARLY_TILES):
+            out0_passes(early_banks[j], 0, j, range(last))
         results = [new_result() for k in range(2)]
         for j in range(TILES):
-            out1_pair(TILES * last + j, (on_scalar, on_vector if j < 2 else on_scalar))
-            if j >= 2:
-                quantize_weight(*turned_late[j - 2])
-            out0_tile(0, j, results[j // 2], on_vector)
+            out1_pair(TILES * last + j)
+            if j >= TILES - len(turned):
+                quantize_weight(*turned.pop(0))
+            if j < EARLY_TILES:
+                tile_bank = early_banks[j]
+                out0_passes(tile_bank, 0, j, [last])
+            else:
+                tile_bank = new_bank()
+                out0_passes(tile_bank, 0, j, range(H))
+            on_vector(out=results[j // 2][:, j % 2, :], in_=tile_bank[:])
             if j % 2 == 1:
                 nc.sync.dma_start(out=out0_hbm[:, j - 1 : j + 1, 0:N], in_=results[j // 2][:])
         results = [new_result() for k in range(2)]
         for j in range(TILES):
-            out0_tile(1, j, results[j // 2], (on_vector, on_scalar)[j % 2])
+            tile_bank = new_bank()
+            out0_passes(tile_bank, 1, j, range(H))
+            (on_vector, on_scalar)[j % 2](out=results[j // 2][:, j % 2, :], in_=tile_bank[:])
             nc.sync.dma_start(out=out0_hbm[:, j, N:E], in_=results[j // 2][:, j % 2, :])

from contextlib import ExitStack

import concourse.mybir as mybir
from concourse.masks import make_identity

T, E, H, DV = 512, 1024, 4, 512
F = H * DV
FLOPS = 3 * 2 * T * E * F

F32 = mybir.dt.float32
BF16 = mybir.dt.bfloat16
U32 = mybir.dt.uint32
U8 = mybir.dt.uint8
E4M3 = mybir.dt.float8_e4m3fn_x4
E5M2 = mybir.dt.float8_e5m2_x4
MULT = mybir.AluOpType.mult

P = 128
N = 512
BANKS = 8
TILES = 4
STEPS = H * TILES
GATE_LEAD = 2
OUT1_START = 6
X_COPY_STEPS = (1, 3)
X_QUANT_STEPS = (4, 5)
EARLY_TILES = 2

RAW_BUFS = 16
STAGE_BUFS = 11
RESULT_BUFS = 9


def tile_multiscaleretention_pc_v_kernel(tc, o_ret, x, Wg, gn_weight, Wo, rstd, grad_out, out_0, out_1):
    nc = tc.nc
    o_hbm = o_ret.rearrange("b (p j) h d -> p (b j) h d", j=TILES)
    x_hbm = x.rearrange("b (p j) e -> p (b j) e", j=TILES)
    go_hbm = grad_out.rearrange("b (p j) e -> p (b j) e", j=TILES)
    rstd_hbm = rstd.rearrange("b (p j) h -> p (b j h)", j=TILES)
    out0_hbm = out_0.rearrange("b (p j) e -> p (b j) e", j=TILES)
    gn_hbm = gn_weight.rearrange("(p c) -> p c", c=4)
    wo_hbm = Wo.rearrange("(h p c) e -> p h c e", p=P, c=4)
    wg_hbm = Wg.rearrange("(i p) f -> p i f", p=P)
    out1_hbm = out_1.rearrange("(i p) f -> p i f", p=P)
    on_scalar, on_vector = nc.scalar.copy, nc.vector.tensor_copy
    whole = slice(0, N)
    last = H - 1

    with ExitStack() as ctx:
        keep = ctx.enter_context(tc.tile_pool(name="keep", bufs=1))
        flow = ctx.enter_context(tc.tile_pool(name="flow", bufs=2))
        psum = ctx.enter_context(tc.psum_pool(name="psum", bufs=1))
        ctx.enter_context(tc.manual_schedule())

        banks_taken = []

        def new_bank():
            tag = "bank%d" % (len(banks_taken) % BANKS)
            banks_taken.append(tag)
            return psum.tile([P, N], F32, name="bank", tag=tag)

        def new_stage():
            return flow.tile([P, 4 * N], BF16, name="stage", tag="stage", bufs=STAGE_BUFS, align_bytes=64)

        def new_result():
            return flow.tile([P, 2, N], F32, name="result", tag="result", bufs=RESULT_BUFS)

        def new_mx(pool, name, width, bufs):
            codes = pool.tile([P, width], U32, name=name + "_codes", tag=name + "_codes", bufs=bufs, align_bytes=64)
            scales = pool.tile([P, width], U8, name=name + "_scales", tag=name + "_scales", bufs=bufs, align_bytes=64)
            return codes, scales

        def load(src):
            raw = flow.tile(list(src.shape), BF16, name="raw", tag="raw", bufs=RAW_BUFS, align_bytes=64)
            nc.sync.dma_start(out=raw[:], in_=src)
            return raw

        def load_wo(h):
            return [load(wo_hbm[:, h, 2 * a : 2 * a + 2, :]) for a in range(2)]

        def load_wg(q):
            rows, cols = 4 * (q // 2), 2 * N * (q % 2)
            return [load(wg_hbm[:, rows + 2 * a : rows + 2 * a + 2, cols : cols + 2 * N]) for a in range(2)]

        def quantize(values, mx, cols, fmt):
            nc.vector.quantize_mx(out=mx[0][:, cols].bitcast(fmt), scales=mx[1][:, cols], in_=values)

        def product(bank, lhs, block, lhs_fmt, rhs, rhs_fmt, start, stop):
            cols = slice(P * block, P * (block + 1))
            nc.tensor.matmul_mx(
                out=bank[:],
                lhsT=lhs[0][:, cols].bitcast(lhs_fmt),
                lhsT_scale=lhs[1][:, cols],
                rhs=rhs[0][:].bitcast(rhs_fmt),
                rhs_scale=rhs[1][:],
                start=start,
                stop=stop,
            )

        def bank_to_stage(bank, stage, a, order, copy):
            half_stage = stage[:].bitcast(F32)[:, N * a : N * (a + 1)]
            copy(
                out=half_stage.rearrange("p (%s u) -> p %s u" % (order, order), s=2, u=2),
                in_=bank[:].rearrange("p (s u r) -> p %s u" % order, s=2, u=2),
            )

        def turn_rows(raw, g, stage, a, order, copy):
            words = raw[:].rearrange("p s k -> p (s k)").bitcast(F32)
            bank = new_bank()
            for s in range(2):
                for u in range(2):
                    first = N * s + 2 * P * g
                    block = slice(P * (2 * s + u), P * (2 * s + u + 1))
                    nc.tensor.transpose(bank[:, block], words[:, first + u : first + 2 * P : 2], ident[:])
            bank_to_stage(bank, stage, a, order, copy)

        def turn_weight(kind, q, g):
            stage = new_stage()
            for a in range(2):
                if kind == "wo":
                    turn_rows(wo_raw[q][a], g, stage, a, "r s", on_scalar)
                else:
                    turn_rows(wg_raw[q][a], g, stage, a, "s r", on_scalar)
            turned.append((kind, q, g, stage))

        def quantize_weight(kind, q, g, stage):
            if kind == "wo":
                mx = wo_mx[q, g] = new_mx(flow, "wo", N, 4)
            else:
                mx = wg_mx[q // 2][2 * (q % 2) + g]
            quantize(stage[:], mx, whole, E4M3)

        def turn_dg(h, a):
            words = dg[h][:].rearrange("p j n -> p (j n)").bitcast(F32)
            bank = new_bank()
            for b in range(4):
                nc.tensor.transpose(bank[:, P * b : P * (b + 1)], words[:, N * a + P * b : N * a + P * (b + 1)], ident[:])
            bank_to_stage(bank, dg_f_stage[h], a, "s r", on_scalar)

        def interleave(tiles, copy):
            stage = new_stage()
            copy(out=stage[:].rearrange("p (c i j) -> p c j i", i=4, j=TILES), in_=tiles.rearrange("p j (c i) -> p c j i", i=4))
            return stage

        def make_gate(step):
            h, j = divmod(step, TILES)
            gate[step] = flow.tile([P, N], F32, name="gate", tag="gate", bufs=GATE_LEAD + 2)
            nc.vector.tensor_tensor(
                out=gate[step][:].rearrange("p (u m e) -> p u m e", u=2, e=2),
                in0=o_raw[h][:, j, :].rearrange("p (m u e) -> p u m e", u=2, e=2),
                in1=gn_row[:].rearrange("p (u m e) -> p u m e", u=2, e=2),
                op=MULT,
            )

        def make_dg(step):
            h, j = divmod(step, TILES)
            bank = new_bank()
            for g in range(2):
                product(bank, go_mx[g], j, E5M2, wo_mx[h, g], E4M3, g == 0, g == 1)
            scale = rstd_sb[:, H * j + h : H * j + h + 1]
            nc.vector.scalar_tensor_tensor(out=dg[h][:, j, :], in0=bank[:], scalar=scale, in1=gate[step][:], op0=MULT, op1=MULT)

        def quantize_dg_tokens(h):
            dg_t_mx[h] = new_mx(flow, "dg_t", N, 2)
            quantize(dg_t_stage[h][:], dg_t_mx[h], whole, E5M2)

        def out1_pair(pair):
            h, k = divmod(pair, 4)
            result = new_result()
            for i in range(2):
                bank = new_bank()
                product(bank, x_mx, 2 * k + i, E4M3, dg_t_mx[h], E5M2, True, True)
                on_scalar(
                    out=result[:, i, :].rearrange("p (m u e) -> p m u e", u=2, e=2),
                    in_=bank[:].rearrange("p (u m e) -> p m u e", u=2, e=2),
                )
            nc.sync.dma_start(out=out1_hbm[:, 2 * k : 2 * k + 2, N * h : N * (h + 1)], in_=result[:])

        def out0_passes(bank, half, j, heads):
            for h in heads:
                product(bank, dg_f_mx[h], j, E5M2, wg_mx[half][h], E4M3, h == 0, h == last)

        gn_col = keep.tile([P, 4], BF16, name="gn_col")
        nc.sync.dma_start(out=gn_col[:], in_=gn_hbm)
        wo_raw, wg_raw, o_raw, go_raw = {0: []}, {}, {}, []
        for a in range(2):
            wo_raw[0].append(load(wo_hbm[:, 0, 2 * a : 2 * a + 2, :]))
            go_raw.append(load(go_hbm[:, 2 * a : 2 * a + 2, :]))
        rstd_sb = keep.tile([P, TILES * H], F32, name="rstd_sb")
        nc.sync.dma_start(out=rstd_sb[:], in_=rstd_hbm)
        o_raw[0] = load(o_hbm[:, :, 0, :])
        wo_raw[1] = load_wo(1)
        o_raw[1] = load(o_hbm[:, :, 1, :])
        x_raw = keep.tile([P, TILES, E], BF16, name="x_raw", align_bytes=64)
        nc.sync.dma_start(out=x_raw[:], in_=x_hbm)
        wo_raw[2] = load_wo(2)
        wg_raw[0] = load_wg(0)

        ident = keep.tile([P, P], F32, name="ident")
        make_identity(nc, ident[:])

        gn_f32 = keep.tile([P, 4], F32, name="gn_f32")
        nc.scalar.copy(out=gn_f32[:], in_=gn_col[:])
        gn_row = keep.tile([P, N], F32, name="gn_row")
        gn_bank = new_bank()
        for c in range(4):
            nc.tensor.transpose(gn_bank[:, P * c : P * (c + 1)], gn_f32[:, c : c + 1].to_broadcast([P, P]), ident[:])
        nc.vector.tensor_copy(
            out=gn_row[:].rearrange("p (u m e) -> p u m e", u=2, e=2),
            in_=gn_bank[:].rearrange("p (u e m) -> p u m e", u=2, e=2),
        )

        go_mx = [new_mx(keep, "go%d" % g, N, 1) for g in range(2)]
        x_mx = new_mx(keep, "x", E, 1)
        wg_mx = [[new_mx(keep, "wg%d_%d" % (half, h), N, 1) for h in range(H)] for half in range(2)]
        dg_f_mx = [new_mx(keep, "dg_f%d" % h, N, 1) for h in range(H)]
        wo_mx, dg_t_mx, dg, gate, dg_f_stage, dg_t_stage, x_stage = {}, {}, {}, {}, {}, {}, {}

        wo_stage = [new_stage() for g in range(2)]
        go_stage = [new_stage() for g in range(2)]

        def quantize_go(a, g):
            quantize(go_stage[g][:, 2 * N * a : 2 * N * (a + 1)], go_mx[g], slice(2 * P * a, 2 * P * (a + 1)), E5M2)

        for g in range(2):
            turn_rows(wo_raw[0][0], g, wo_stage[g], 0, "r s", (on_scalar, on_vector)[g])
        for g in range(2):
            turn_rows(go_raw[0], g, go_stage[g], 0, "s r", (on_scalar, on_vector)[g])
        for g in range(2):
            turn_rows(wo_raw[0][1], g, wo_stage[g], 1, "r s", on_scalar)
            quantize_go(0, g)
        for g in range(2):
            turn_rows(go_raw[1], g, go_stage[g], 1, "s r", on_scalar)
            quantize_weight("wo", 0, g, wo_stage[g])
        for step in range(GATE_LEAD):
            make_gate(step)
        o_raw[2] = load(o_hbm[:, :, 2, :])
        wo_raw[3] = load_wo(3)
        wg_raw[1] = load_wg(1)
        o_raw[3] = load(o_hbm[:, :, 3, :])
        wg_raw[2] = load_wg(2)

        blocks = [("wo", 1), None, ("wo", 2), ("wg", 0), ("wo", 3), ("wg", 1), ("wg", 2), ("wg", 3)]
        turned = []
        for step in range(STEPS):
            h, j = divmod(step, TILES)
            if step == TILES:
                wg_raw[last] = load_wg(last)
            if j == 0:
                dg[h] = flow.tile([P, TILES, N], BF16, name="dg", tag="dg", bufs=2, align_bytes=64)
            make_dg(step)
            if step < 2:
                quantize_go(1, step)
            if j == 0 and h > 0:
                quantize_dg_tokens(h - 1)
            if step in X_QUANT_STEPS:
                half = X_QUANT_STEPS.index(step)
                quantize(x_stage[half][:], x_mx, slice(N * half, N * (half + 1)), E4M3)
            if turned and step < STEPS - 1:
                quantize_weight(*turned.pop(0))
            if step + GATE_LEAD < STEPS:
                make_gate(step + GATE_LEAD)
            if j == 2 and h > 0:
                quantize(dg_f_stage[h - 1][:], dg_f_mx[h - 1], whole, E5M2)
            if step >= OUT1_START:
                out1_pair(step - OUT1_START)
            if j == TILES - 1:
                dg_t_stage[h] = interleave(dg[h][:], on_vector)
            if blocks[step // 2]:
                turn_weight(*blocks[step // 2], step % 2)
            if j == 2:
                dg_f_stage[h] = new_stage()
                turn_dg(h, 0)
            if j == 0 and h > 0:
                turn_dg(h - 1, 1)
            if step in X_COPY_STEPS:
                half = X_COPY_STEPS.index(step)
                x_stage[half] = interleave(x_raw[:, :, N * half : N * (half + 1)], on_scalar)

        turn_dg(last, 1)
        quantize_dg_tokens(last)
        quantize(dg_f_stage[last][:], dg_f_mx[last], whole, E5M2)
        for pair in range(STEPS - OUT1_START, TILES * last):
            out1_pair(pair)
        early_banks = [new_bank() for j in range(EARLY_TILES)]
        for j in range(EARLY_TILES):
            out0_passes(early_banks[j], 0, j, range(last))
        results = [new_result() for k in range(2)]
        for j in range(TILES):
            out1_pair(TILES * last + j)
            if j >= TILES - len(turned):
                quantize_weight(*turned.pop(0))
            if j < EARLY_TILES:
                tile_bank = early_banks[j]
                out0_passes(tile_bank, 0, j, [last])
            else:
                tile_bank = new_bank()
                out0_passes(tile_bank, 0, j, range(H))
            on_vector(out=results[j // 2][:, j % 2, :], in_=tile_bank[:])
            if j % 2 == 1:
                nc.sync.dma_start(out=out0_hbm[:, j - 1 : j + 1, 0:N], in_=results[j // 2][:])
        results = [new_result() for k in range(2)]
        for j in range(TILES):
            tile_bank = new_bank()
            out0_passes(tile_bank, 1, j, range(H))
            (on_vector, on_scalar)[j % 2](out=results[j // 2][:, j % 2, :], in_=tile_bank[:])
            nc.sync.dma_start(out=out0_hbm[:, j, N:E], in_=results[j // 2][:, j % 2, :])
